import numpy as np
import ml_dtypes


def mxq(x, axis, fmt="e4m3"):
    dtype, down = {"e4m3": (ml_dtypes.float8_e4m3fn, 7), "e5m2": (ml_dtypes.float8_e5m2, 14)}[fmt]
    v = np.moveaxis(np.asarray(x, np.float32).astype(ml_dtypes.bfloat16).astype(np.float64), axis, -1)
    blocks = v.reshape(v.shape[:-1] + (-1, 32))
    amax = np.abs(blocks).max(-1, keepdims=True)
    byte = np.maximum(np.where(amax > 0, np.frexp(amax)[1] - 1 + 127, 0) - down, 1)
    scale = np.exp2(byte - 127.0)
    codes = (blocks / scale).astype(np.float32).astype(dtype).astype(np.float64)
    return np.moveaxis((codes * scale).reshape(v.shape), -1, axis)


WIDE = False


def mx_kscale(k):
    if not WIDE:
        return np.ones(k)
    levels = np.array([10, -10, 5, -5, 0])
    a = np.random.permutation(np.resize(levels, k // 512 * 4)).reshape(k // 512, 4)
    idx = np.arange(k)
    return np.exp2(a[idx // 512, idx % 128 // 32])


BF16 = ml_dtypes.bfloat16


def bf(x):
    return np.asarray(x, np.float32).astype(BF16)


def f64(x):
    return np.asarray(x).astype(np.float64)


E2M1 = np.array([0.0, 0.5, 1.0, 1.5, 2.0, 3.0, 4.0, 6.0, -0.0, -0.5, -1.0, -1.5, -2.0, -3.0, -4.0, -6.0])


def pack_weight(w, fmt):
    k, n = w.shape
    w = f64(bf(w)).reshape(k // 32, 32, n)
    amax = np.abs(w).max(1)
    if fmt == "e4m3":
        byte = np.frexp(amax)[1] - 1 + 127 - 7
    else:
        mant, ex = np.frexp(amax / 6.0)
        byte = np.where(mant > 0.5, ex, ex - 1) + 127
    byte = np.clip(np.where(amax > 0, byte, 1), 1, 254)
    scaled = (w * np.exp2(127.0 - byte)[:, None, :]).reshape(k, n).astype(np.float32)
    by_word = np.ascontiguousarray(scaled.reshape(k // 512, 128, 4, n).transpose(0, 1, 3, 2))
    if fmt == "e4m3":
        words = by_word.astype(ml_dtypes.float8_e4m3fn).view(np.uint8)
    else:
        c = by_word.astype(ml_dtypes.float4_e2m1fn).view(np.uint8) & 0xF
        words = c[..., 0::2] | (c[..., 1::2] << 4)
    return np.ascontiguousarray(words), np.ascontiguousarray(byte.astype(np.uint8).reshape(k // 512, 16, n))


def unpack_weight(words, scales, fmt):
    g, p, n, _ = words.shape
    if fmt == "e4m3":
        vals = np.ascontiguousarray(words).view(ml_dtypes.float8_e4m3fn).astype(np.float64)
    else:
        nib = np.empty((g, p, n, 4), np.uint8)
        nib[..., 0::2] = words & 0xF
        nib[..., 1::2] = words >> 4
        vals = E2M1[nib]
    vals = vals * np.repeat(np.exp2(scales.astype(np.float64) - 127.0), 8, axis=1)[..., None]
    return vals.transpose(0, 1, 3, 2).reshape(g * 512, n)


B, H, W, D, Dh, Dq, R, T = 4, 8, 8, 8192, 1024, 128, 16, 8
EPS = 1e-6
FMT = "e4m3"


def layer_norm(v, g, b):
    mu = v.mean(-1, keepdims=True)
    var = ((v - mu) ** 2).mean(-1, keepdims=True)
    return (v - mu) / np.sqrt(var + EPS) * g + b


def setup_inputs():
    rn = np.random.standard_normal
    s, t = mx_kscale(D), mx_kscale(Dh)
    x = bf(rn((B, H, W, D)) * s)
    z2 = bf(rn((B, H, W, Dq)) * 1.5)
    U1_w_words, U1_w_scales = pack_weight(np.ascontiguousarray((rn((Dh, D)) * np.sqrt(2.0 / D) / s).T), FMT)
    U1_b = bf(rn(Dh) * 0.5)
    U3_w = bf(rn((Dh, Dq)) * np.sqrt(2.0 / Dq))
    U3_b = bf(rn(Dh) * 0.5)
    C_w_words, C_w_scales = pack_weight(np.ascontiguousarray((rn((D, Dh)) / np.sqrt(Dh) / t).T), FMT)
    return {
        "x": x,
        "z2": z2,
        "U1_w_words": U1_w_words,
        "U1_w_scales": U1_w_scales,
        "U1_b": U1_b,
        "U3_w": U3_w,
        "U3_b": U3_b,
        "C_w_words": C_w_words,
        "C_w_scales": C_w_scales,
        "C_b": bf(rn(D) * 0.3),
        "ln1_g": bf((1.0 + 0.1 * rn(Dh)) * t),
        "ln1_b": bf(0.2 * rn(Dh) * t),
        "ln3_g": bf(1.0 + 0.1 * rn(Dh)),
        "ln3_b": bf(0.2 * rn(Dh)),
        "alpha": bf(0.6 + 0.2 * np.random.random(1)),
    }


def reference(x, z2, U1_w_words, U1_w_scales, U1_b, U3_w, U3_b, C_w_words, C_w_scales, C_b, ln1_g, ln1_b, ln3_g, ln3_b, alpha):
    out1 = (mxq(f64(x), 3, "e4m3") @ unpack_weight(U1_w_words, U1_w_scales, FMT)) + f64(U1_b)
    out3 = f64(z2) @ f64(U3_w).T + f64(U3_b)
    o1 = layer_norm(out1, f64(ln1_g), f64(ln1_b))
    o3 = layer_norm(out3, f64(ln3_g), f64(ln3_b))
    h = o1 + f64(alpha) * (o1 * o3)
    return (mxq(h, 3, "e4m3") @ unpack_weight(C_w_words, C_w_scales, FMT)) + f64(C_b)

@@ -1,0 +1,369 @@
+from contextlib import ExitStack
+
+import concourse.mybir as mybir
+from concourse.masks import make_identity
+
+F32 = mybir.dt.float32
+BF16 = mybir.dt.bfloat16
+I32 = mybir.dt.int32
+U32 = mybir.dt.uint32
+U8 = mybir.dt.uint8
+FP8X4 = mybir.dt.float8_e4m3fn_x4
+ALU = mybir.AluOpType
+ACT = mybir.ActivationFunctionType
+
+P = 128
+TOKEN_TILES = 2
+D = 8192
+DH = 1024
+DQ = 128
+EPS = 1e-6
+K_PASS = 512
+G1 = D // K_PASS
+G2 = DH // K_PASS
+BANK = 512
+HALVES = DH // BANK
+RING_COLS = 2048
+QUARTERS = D // RING_COLS
+TILES_PER_QUARTER = RING_COLS // BANK
+OUT_TILES = D // BANK
+
+ROW_U3_B = 0
+ROW_LN3_G = 1
+ROW_LN3_B = 2
+ROW_U1_B = 0
+ROW_LN1_G = 1
+ROW_LN1_B = 2
+ROW_C_B = 3
+
+BIAS_AHEAD = 8
+
+FLOPS = 2 * P * TOKEN_TILES * (D * DH + DQ * DH + DH * D)
+
+
+def tile_polymlp_skiplora_pa_k_kernel(
+    tc, x, z2, U1_w_words, U1_w_scales, U1_b, U3_w, U3_b, C_w_words, C_w_scales, C_b,
+    ln1_g, ln1_b, ln3_g, ln3_b, alpha, out,
+):
+    nc = tc.nc
+    x_rows = x.flatten_outer_dims()
+    z2_rows = z2.flatten_outer_dims()
+    out_rows = out.flatten_outer_dims()
+
+    with ExitStack() as stack:
+        stack.enter_context(tc.manual_schedule())
+        keep = stack.enter_context(tc.tile_pool(name="keep", bufs=1))
+        per_token_tile = stack.enter_context(tc.tile_pool(name="per_token_tile", bufs=TOKEN_TILES))
+        stage = stack.enter_context(tc.tile_pool(name="stage", bufs=3))
+        small = stack.enter_context(tc.tile_pool(name="small", bufs=4))
+        ring = stack.enter_context(tc.tile_pool(name="ring", bufs=16))
+        psum = stack.enter_context(tc.psum_pool(name="psum", bufs=4))
+
+        rows3 = keep.tile([P, DH], BF16)
+        nc.vector.memset(rows3[:].bitcast(I32), 0)
+        rows1 = keep.tile([P, DH], BF16)
+        nc.vector.memset(rows1[:].bitcast(I32), 0)
+        u1_planes = keep.tile([P, G1 // 4, DH], U8, align_bytes=64)
+        nc.vector.memset(u1_planes[:].rearrange("p j n -> p (j n)").bitcast(I32), 0)
+        c_planes = keep.tile([P, G2, RING_COLS], U8, align_bytes=64)
+        nc.vector.memset(c_planes[:].rearrange("p g n -> p (g n)").bitcast(I32), 0)
+        eps = keep.tile([P, 1], F32)
+        nc.vector.memset(eps[:], EPS)
+        ident_bf = keep.tile([P, P], BF16)
+        make_identity(nc, ident_bf[:])
+        ident_f32 = keep.tile([P, P], F32)
+        make_identity(nc, ident_f32[:])
+
+        def load_row(queue, rows, row, vector):
+            queue.dma_start(out=rows[row : row + 1, :], in_=vector.rearrange("(o n) -> o n", o=1))
+
+        u3_raw = keep.tile([P, DH // P, DQ], BF16)
+        nc.scalar.dma_start(out=u3_raw[:], in_=U3_w.rearrange("(p a) k -> p a k", a=DH // P))
+        z2_raw = keep.tile([P, TOKEN_TILES, DQ], BF16)
+        nc.scalar.dma_start(out=z2_raw[:], in_=z2_rows.rearrange("(m p) k -> p m k", p=P))
+        load_row(nc.scalar, rows3, ROW_U3_B, U3_b)
+        load_row(nc.scalar, rows3, ROW_LN3_G, ln3_g)
+        load_row(nc.scalar, rows3, ROW_LN3_B, ln3_b)
+        alpha_bf = keep.tile([P, 1], BF16)
+        nc.scalar.dma_start(out=alpha_bf[:], in_=alpha.partition_broadcast(P))
+        load_row(nc.gpsimd, rows1, ROW_U1_B, U1_b)
+        load_row(nc.gpsimd, rows1, ROW_LN1_G, ln1_g)
+        load_row(nc.gpsimd, rows1, ROW_LN1_B, ln1_b)
+        nc.gpsimd.dma_start(
+            out=rows1[ROW_C_B : ROW_C_B + D // DH, :], in_=C_b.rearrange("(r n) -> r n", n=DH)
+        )
+
+        x_tiles = {}
+        u1_tiles = []
+        c_tiles = {}
+
+        def load_x_half(half):
+            for m in range(TOKEN_TILES):
+                x_tile = ring.tile([P, 2 * RING_COLS], BF16, tag="ring", name="x_%d_%d" % (half, m), align_bytes=64)
+                nc.sync.dma_start(
+                    out=x_tile[:],
+                    in_=x_rows[P * m : P * (m + 1), 2 * RING_COLS * half : 2 * RING_COLS * (half + 1)],
+                )
+                x_tiles[(half, m)] = x_tile
+
+        def load_u1_planes(j):
+            for quadrant in range(4):
+                nc.sync.dma_start(
+                    out=u1_planes[32 * quadrant : 32 * quadrant + 16, j, :].bitcast(I32),
+                    in_=U1_w_scales[4 * j : 4 * j + 4, 4 * quadrant : 4 * quadrant + 4, :].bitcast(I32),
+                )
+
+        def load_u1_words(a):
+            u1_tile = ring.tile([P, 2, DH], U32, tag="ring", name="u1_%d" % a, align_bytes=64)
+            nc.sync.dma_start(
+                out=u1_tile[:].bitcast(I32),
+                in_=U1_w_words[2 * a : 2 * a + 2].rearrange("g p n t -> p g (n t)").bitcast(I32),
+            )
+            u1_tiles.append(u1_tile)
+
+        def load_c_planes(g):
+            for quadrant in range(4):
+                nc.sync.dma_start(
+                    out=c_planes[32 * quadrant : 32 * quadrant + 16, g, :].bitcast(I32),
+                    in_=C_w_scales[g, 4 * quadrant : 4 * quadrant + 4, :]
+                    .rearrange("r (c n) -> c r n", c=QUARTERS)
+                    .bitcast(I32),
+                )
+
+        def load_c_words(c):
+            for g in range(G2):
+                c_tile = ring.tile([P, RING_COLS], U32, tag="ring", name="c_%d_%d" % (c, g), align_bytes=64)
+                nc.sync.dma_start(
+                    out=c_tile[:].bitcast(I32),
+                    in_=C_w_words[g, :, RING_COLS * c : RING_COLS * (c + 1), :]
+                    .rearrange("p n t -> p (n t)")
+                    .bitcast(I32),
+                )
+                c_tiles[(c, g)] = c_tile
+
+        for half in range(2):
+            load_x_half(half)
+            load_u1_planes(half)
+        for j in range(G1 // 4):
+            load_u1_words(2 * j)
+            load_u1_words(2 * j + 1)
+            if j < 2:
+                load_u1_planes(j + 2)
+            else:
+                load_c_planes(j - 2)
+        load_c_words(0)
+        load_c_words(1)
+
+        def spread_row(rows, row, columns):
+            bank = psum.tile([P, BANK], F32, tag="work")
+            nc.tensor.matmul(
+                bank[:], lhsT=ident_bf[:, row : row + 1].to_broadcast([P, P]), rhs=rows[:, columns],
+                start=True, stop=True,
+            )
+            return bank
+
+        def half_cols(hf):
+            return slice(BANK * hf, BANK * (hf + 1))
+
+        def norm_first(y, gain):
+            stats = small.tile([P, HALVES, 6], F32)
+            for hf in range(HALVES):
+                nc.vector.bn_stats(out=stats[:, hf, :], in_=y[:, half_cols(hf)])
+            mean_var = small.tile([P, 2], F32)
+            nc.vector.bn_aggr(out=mean_var[:], in_=stats[:].rearrange("p a s -> p (a s)"))
+            std = small.tile([P, 1], F32)
+            nc.scalar.activation(out=std[:], in_=mean_var[:, 1:2], func=ACT.Sqrt, bias=eps[:, 0:1], scale=1.0)
+            nc.vector.scalar_tensor_tensor(
+                out=y[:], in0=y[:], scalar=mean_var[:, 0:1], in1=gain[:], op0=ALU.subtract, op1=ALU.mult
+            )
+            return std
+
+        def norm_second(y, std, shift, result):
+            rstd = small.tile([P, 1], F32)
+            nc.vector.reciprocal(out=rstd[:], in_=std[:])
+            nc.vector.scalar_tensor_tensor(
+                out=result[:], in0=y[:], scalar=rstd[:, 0:1], in1=shift[:], op0=ALU.mult, op1=ALU.add
+            )
+
+        u3_bank = psum.tile([P, DH // P, P], BF16, tag="work")
+        for a in range(DH // P):
+            nc.tensor.transpose(u3_bank[:, a, :], u3_raw[:, a, :], ident_bf[:])
+        u3_t = keep.tile([P, DH], BF16)
+        nc.vector.tensor_copy(
+            out=u3_t[:].rearrange("k (p a) -> k p a", a=DH // P), in_=u3_bank[:].rearrange("k a p -> k p a")
+        )
+        z2_bank = psum.tile([P, TOKEN_TILES, P], BF16, tag="work")
+        for m in range(TOKEN_TILES):
+            nc.tensor.transpose(z2_bank[:, m, :], z2_raw[:, m, :], ident_bf[:])
+        z2_t = keep.tile([P, TOKEN_TILES, P], BF16)
+        nc.vector.tensor_copy(out=z2_t[:], in_=z2_bank[:])
+
+        alpha_f32 = keep.tile([P, 1], F32)
+        nc.vector.tensor_copy(out=alpha_f32[:], in_=alpha_bf[:])
+        gate_gain = keep.tile([P, DH], F32)
+        gate_shift = keep.tile([P, DH], F32)
+        for hf in range(HALVES):
+            bank = spread_row(rows3, ROW_LN3_G, half_cols(hf))
+            nc.vector.tensor_scalar(
+                out=gate_gain[:, half_cols(hf)], in0=bank[:], scalar1=alpha_f32[:, 0:1], scalar2=None, op0=ALU.mult
+            )
+        for hf in range(HALVES):
+            bank = spread_row(rows3, ROW_LN3_B, half_cols(hf))
+            nc.vector.tensor_scalar(
+                out=gate_shift[:, half_cols(hf)], in0=bank[:], scalar1=alpha_f32[:, 0:1], scalar2=1.0,
+                op0=ALU.mult, op1=ALU.add,
+            )
+
+        gates = []
+        for m in range(TOKEN_TILES):
+            gate = per_token_tile.tile([P, DH], F32, name="gate_%d" % m, tag="gate")
+            for hf in range(HALVES):
+                bank = psum.tile([P, BANK], F32, tag="work")
+                nc.tensor.matmul(bank[:], lhsT=z2_t[:, m, :], rhs=u3_t[:, half_cols(hf)], start=True, stop=False)
+                nc.tensor.matmul(
+                    bank[:], lhsT=ident_bf[:, ROW_U3_B : ROW_U3_B + 1].to_broadcast([P, P]),
+                    rhs=rows3[:, half_cols(hf)], start=False, stop=True,
+                )
+                nc.scalar.copy(out=gate[:, half_cols(hf)], in_=bank[:])
+            gates.append(gate)
+
+        x_codes = keep.tile([P, TOKEN_TILES, G1 * P], U32, tag="codes_then_bias", align_bytes=64)
+        x_planes = keep.tile([P, TOKEN_TILES, G1 * P], U8, align_bytes=64)
+        groups_per_x_tile = G1 // 2
+        for half in range(2):
+            for m in range(TOKEN_TILES):
+                x_words = x_tiles[(half, m)][:].bitcast(F32)
+                for pair in range(groups_per_x_tile // 2):
+                    bank = psum.tile([P, 2, 2, P], F32, tag="work")
+                    for a in range(2):
+                        for u in range(2):
+                            first = 256 * (2 * pair + a)
+                            nc.tensor.transpose(bank[:, a, u, :], x_words[:, first + u : first + 256 : 2], ident_f32[:])
+                    grouped = stage.tile([P, 2 * P * 4], BF16, align_bytes=64)
+                    nc.scalar.copy(
+                        out=grouped[:].bitcast(F32).rearrange("p (a r u) -> p a r u", a=2, u=2),
+                        in_=bank[:].rearrange("p a u r -> p a r u"),
+                    )
+                    g = groups_per_x_tile * half + 2 * pair
+                    nc.vector.quantize_mx(
+                        out=x_codes[:, m, P * g : P * (g + 2)].bitcast(FP8X4),
+                        scales=x_planes[:, m, P * g : P * (g + 2)],
+                        in_=grouped[:],
+                    )
+
+        load_c_words(2)
+        load_c_words(3)
+
+        spread = {}
+        for row in (ROW_U1_B, ROW_LN1_G, ROW_LN1_B):
+            spread[row] = keep.tile([P, DH], BF16, name="spread_%d" % row)
+            for hf in range(HALVES):
+                bank = spread_row(rows1, row, half_cols(hf))
+                nc.scalar.copy(out=spread[row][:, half_cols(hf)], in_=bank[:])
+
+        h_gains = []
+        h_shifts = []
+        for m in range(TOKEN_TILES):
+            gate = gates[m]
+            std = norm_first(gate, gate_gain)
+            norm_second(gate, std, gate_shift, gate)
+            h_gain = per_token_tile.tile([P, DH], F32, name="h_gain_%d" % m, tag="h_gain")
+            nc.vector.tensor_tensor(out=h_gain[:], in0=gate[:], in1=spread[ROW_LN1_G][:], op=ALU.mult)
+            nc.vector.tensor_tensor(out=gate[:], in0=gate[:], in1=spread[ROW_LN1_B][:], op=ALU.mult)
+            h_gains.append(h_gain)
+            h_shifts.append(gate)
+
+        sums1 = {}
+        for m in range(TOKEN_TILES):
+            for hf in range(HALVES):
+                sums1[(m, hf)] = psum.tile([P, BANK], F32, tag="sums", name="sums1_%d_%d" % (m, hf))
+        for g in range(G1):
+            for m in range(TOKEN_TILES):
+                for hf in range(HALVES):
+                    nc.tensor.matmul_mx(
+                        out=sums1[(m, hf)][:],
+                        lhsT=x_codes[:, m, P * g : P * (g + 1)].bitcast(FP8X4),
+                        lhsT_scale=x_planes[:, m, P * g : P * (g + 1)],
+                        rhs=u1_tiles[g // 2][:, g % 2, half_cols(hf)].bitcast(FP8X4),
+                        rhs_scale=u1_planes[4 * (g % 4) : P, g // 4, half_cols(hf)],
+                        start=(g == 0),
+                        stop=(g == G1 - 1),
+                    )
+
+        bias_all = keep.tile([P, D], BF16, tag="codes_then_bias", align_bytes=64)
+        h_codes = keep.tile([P, TOKEN_TILES, G2 * P], U32, align_bytes=64)
+        h_planes = keep.tile([P, TOKEN_TILES, G2 * P], U8, align_bytes=64)
+
+        def spread_bias(j):
+            bank = spread_row(rows1, ROW_C_B + j // HALVES, half_cols(j % HALVES))
+            nc.scalar.copy(out=bias_all[:, BANK * j : BANK * (j + 1)], in_=bank[:])
+
+        def add_u1_b(m):
+            y1 = per_token_tile.tile([P, DH], F32, name="y1_%d" % m, tag="y1")
+            for hf in range(HALVES):
+                nc.vector.tensor_tensor(
+                    out=y1[:, half_cols(hf)], in0=sums1[(m, hf)][:], in1=spread[ROW_U1_B][:, half_cols(hf)], op=ALU.add
+                )
+            return y1
+
+        def transpose_h(h):
+            bank = psum.tile([P, G2, 4, P], BF16, tag="work")
+            for g in range(G2):
+                for t in range(4):
+                    nc.tensor.transpose(bank[:, g, t, :], h[:, K_PASS * g + t : K_PASS * (g + 1) : 4], ident_bf[:])
+            h_grouped = per_token_tile.tile([P, G2, P, 4], BF16, align_bytes=64)
+            nc.scalar.copy(out=h_grouped[:], in_=bank[:].rearrange("p g t r -> p g r t"))
+            return h_grouped
+
+        def quantise_h(m, h_grouped):
+            nc.vector.quantize_mx(
+                out=h_codes[:, m, :].bitcast(FP8X4),
+                scales=h_planes[:, m, :],
+                in_=h_grouped[:].rearrange("p g r t -> p (g r t)"),
+            )
+
+        def out_quarter(m, c):
+            out_tile = ring.tile([P, RING_COLS], F32, tag="ring", name="out_%d_%d" % (m, c), align_bytes=64)
+            for i in range(TILES_PER_QUARTER):
+                j = TILES_PER_QUARTER * c + i
+                if m == 0 and j + BIAS_AHEAD < OUT_TILES:
+                    spread_bias(j + BIAS_AHEAD)
+                sums2 = psum.tile([P, BANK], F32, tag="sums")
+                for g in range(G2):
+                    nc.tensor.matmul_mx(
+                        out=sums2[:],
+                        lhsT=h_codes[:, m, P * g : P * (g + 1)].bitcast(FP8X4),
+                        lhsT_scale=h_planes[:, m, P * g : P * (g + 1)],
+                        rhs=c_tiles[(c, g)][:, BANK * i : BANK * (i + 1)].bitcast(FP8X4),
+                        rhs_scale=c_planes[4 * c : P, g, BANK * i : BANK * (i + 1)],
+                        start=(g == 0),
+                        stop=(g == G2 - 1),
+                    )
+                nc.vector.tensor_tensor(
+                    out=out_tile[:, BANK * i : BANK * (i + 1)], in0=sums2[:],
+                    in1=bias_all[:, BANK * j : BANK * (j + 1)], op=ALU.add,
+                )
+            nc.sync.dma_start(
+                out=out_rows[P * m : P * (m + 1), RING_COLS * c : RING_COLS * (c + 1)], in_=out_tile[:]
+            )
+
+        y1_0 = add_u1_b(0)
+        std_0 = norm_first(y1_0, h_gains[0])
+        for j in range(BIAS_AHEAD):
+            spread_bias(j)
+        h_0 = per_token_tile.tile([P, DH], BF16, tag="h")
+        norm_second(y1_0, std_0, h_shifts[0], h_0)
+        h_grouped_0 = transpose_h(h_0)
+        y1_1 = add_u1_b(1)
+        std_1 = norm_first(y1_1, h_gains[1])
+        quantise_h(0, h_grouped_0)
+        h_1 = per_token_tile.tile([P, DH], BF16, tag="h")
+        norm_second(y1_1, std_1, h_shifts[1], h_1)
+
+        out_quarter(0, 0)
+        h_grouped_1 = transpose_h(h_1)
+        quantise_h(1, h_grouped_1)
+        for c in range(1, QUARTERS):
+            out_quarter(0, c)
+        for c in range(QUARTERS):
+            out_quarter(1, c)

@@ -38,6 +38,8 @@ ROW_C_B = 3
 
 BIAS_AHEAD = 8
 
+TOKEN_TILE_LAG = 8
+
 FLOPS = 2 * P * TOKEN_TILES * (D * DH + DQ * DH + DH * D)
 
 
@@ -277,18 +279,24 @@ def tile_polymlp_skiplora_pa_k_kernel(
         for m in range(TOKEN_TILES):
             for hf in range(HALVES):
                 sums1[(m, hf)] = psum.tile([P, BANK], F32, tag="sums", name="sums1_%d_%d" % (m, hf))
-        for g in range(G1):
-            for m in range(TOKEN_TILES):
-                for hf in range(HALVES):
-                    nc.tensor.matmul_mx(
-                        out=sums1[(m, hf)][:],
-                        lhsT=x_codes[:, m, P * g : P * (g + 1)].bitcast(FP8X4),
-                        lhsT_scale=x_planes[:, m, P * g : P * (g + 1)],
-                        rhs=u1_tiles[g // 2][:, g % 2, half_cols(hf)].bitcast(FP8X4),
-                        rhs_scale=u1_planes[4 * (g % 4) : P, g // 4, half_cols(hf)],
-                        start=(g == 0),
-                        stop=(g == G1 - 1),
-                    )
+
+        def first_product(m, g):
+            for hf in range(HALVES):
+                nc.tensor.matmul_mx(
+                    out=sums1[(m, hf)][:],
+                    lhsT=x_codes[:, m, P * g : P * (g + 1)].bitcast(FP8X4),
+                    lhsT_scale=x_planes[:, m, P * g : P * (g + 1)],
+                    rhs=u1_tiles[g // 2][:, g % 2, half_cols(hf)].bitcast(FP8X4),
+                    rhs_scale=u1_planes[4 * (g % 4) : P, g // 4, half_cols(hf)],
+                    start=(g == 0),
+                    stop=(g == G1 - 1),
+                )
+
+        for g in range(G1 + TOKEN_TILE_LAG):
+            if g < G1:
+                first_product(0, g)
+            if g >= TOKEN_TILE_LAG:
+                first_product(1, g - TOKEN_TILE_LAG)
 
         bias_all = keep.tile([P, D], BF16, tag="codes_then_bias", align_bytes=64)
         h_codes = keep.tile([P, TOKEN_TILES, G2 * P], U32, align_bytes=64)
@@ -349,13 +357,13 @@ def tile_polymlp_skiplora_pa_k_kernel(
 
         y1_0 = add_u1_b(0)
         std_0 = norm_first(y1_0, h_gains[0])
-        for j in range(BIAS_AHEAD):
-            spread_bias(j)
         h_0 = per_token_tile.tile([P, DH], BF16, tag="h")
         norm_second(y1_0, std_0, h_shifts[0], h_0)
         h_grouped_0 = transpose_h(h_0)
         y1_1 = add_u1_b(1)
         std_1 = norm_first(y1_1, h_gains[1])
+        for j in range(BIAS_AHEAD):
+            spread_bias(j)
         quantise_h(0, h_grouped_0)
         h_1 = per_token_tile.tile([P, DH], BF16, tag="h")
         norm_second(y1_1, std_1, h_shifts[1], h_1)

@@ -56,21 +56,21 @@ def tile_polymlp_skiplora_pa_k_kernel(
         stack.enter_context(tc.manual_schedule())
         keep = stack.enter_context(tc.tile_pool(name="keep", bufs=1))
         per_token_tile = stack.enter_context(tc.tile_pool(name="per_token_tile", bufs=TOKEN_TILES))
-        stage = stack.enter_context(tc.tile_pool(name="stage", bufs=3))
+        stage = stack.enter_context(tc.tile_pool(name="stage", bufs=4))
         small = stack.enter_context(tc.tile_pool(name="small", bufs=4))
         ring = stack.enter_context(tc.tile_pool(name="ring", bufs=16))
         psum = stack.enter_context(tc.psum_pool(name="psum", bufs=4))
 
         rows3 = keep.tile([P, DH], BF16)
         nc.vector.memset(rows3[:].bitcast(I32), 0)
+        eps = keep.tile([P, 1], F32)
+        nc.vector.memset(eps[:], EPS)
         rows1 = keep.tile([P, DH], BF16)
         nc.vector.memset(rows1[:].bitcast(I32), 0)
         u1_planes = keep.tile([P, G1 // 4, DH], U8, align_bytes=64)
         nc.vector.memset(u1_planes[:].rearrange("p j n -> p (j n)").bitcast(I32), 0)
         c_planes = keep.tile([P, G2, RING_COLS], U8, align_bytes=64)
         nc.vector.memset(c_planes[:].rearrange("p g n -> p (g n)").bitcast(I32), 0)
-        eps = keep.tile([P, 1], F32)
-        nc.vector.memset(eps[:], EPS)
         ident_bf = keep.tile([P, P], BF16)
         make_identity(nc, ident_bf[:])
         ident_f32 = keep.tile([P, P], F32)
@@ -88,6 +88,8 @@ def tile_polymlp_skiplora_pa_k_kernel(
         load_row(nc.scalar, rows3, ROW_LN3_B, ln3_b)
         alpha_bf = keep.tile([P, 1], BF16)
         nc.scalar.dma_start(out=alpha_bf[:], in_=alpha.partition_broadcast(P))
+        table_warm = keep.tile([P, 1], F32)
+        nc.scalar.activation(out=table_warm[:], in_=eps[:], func=ACT.Sqrt)
         load_row(nc.gpsimd, rows1, ROW_U1_B, U1_b)
         load_row(nc.gpsimd, rows1, ROW_LN1_G, ln1_g)
         load_row(nc.gpsimd, rows1, ROW_LN1_B, ln1_b)
@@ -99,14 +101,16 @@ def tile_polymlp_skiplora_pa_k_kernel(
         u1_tiles = []
         c_tiles = {}
 
-        def load_x_half(half):
-            for m in range(TOKEN_TILES):
-                x_tile = ring.tile([P, 2 * RING_COLS], BF16, tag="ring", name="x_%d_%d" % (half, m), align_bytes=64)
+        def load_x(half, m, pieces):
+            x_tile = ring.tile([P, 2 * RING_COLS], BF16, tag="ring", name="x_%d_%d" % (half, m), align_bytes=64)
+            width = 2 * RING_COLS // pieces
+            for i in range(pieces):
+                first = 2 * RING_COLS * half + width * i
                 nc.sync.dma_start(
-                    out=x_tile[:],
-                    in_=x_rows[P * m : P * (m + 1), 2 * RING_COLS * half : 2 * RING_COLS * (half + 1)],
+                    out=x_tile[:, width * i : width * (i + 1)],
+                    in_=x_rows[P * m : P * (m + 1), first : first + width],
                 )
-                x_tiles[(half, m)] = x_tile
+            x_tiles[(half, m)] = x_tile
 
         def load_u1_planes(j):
             for quadrant in range(4):
@@ -143,9 +147,10 @@ def tile_polymlp_skiplora_pa_k_kernel(
                 )
                 c_tiles[(c, g)] = c_tile
 
-        for half in range(2):
-            load_x_half(half)
-            load_u1_planes(half)
+        for m in range(TOKEN_TILES):
+            load_x(0, m, 2 if m == 0 else 1)
+            load_x(1, m, 1)
+            load_u1_planes(m)
         for j in range(G1 // 4):
             load_u1_words(2 * j)
             load_u1_words(2 * j + 1)
@@ -187,6 +192,30 @@ def tile_polymlp_skiplora_pa_k_kernel(
                 out=result[:], in0=y[:], scalar=rstd[:, 0:1], in1=shift[:], op0=ALU.mult, op1=ALU.add
             )
 
+        x_codes = keep.tile([P, TOKEN_TILES, G1 * P], U32, tag="codes_then_bias", align_bytes=64)
+        x_planes = keep.tile([P, TOKEN_TILES, G1 * P], U8, align_bytes=64)
+        PAIRS = G1 // 2
+        pairs_per_x_tile = PAIRS // 2
+
+        def x_pair(m, pair):
+            x_words = x_tiles[(pair // pairs_per_x_tile, m)][:].bitcast(F32)
+            bank = psum.tile([P, 2, 2, P], F32, tag="work")
+            for a in range(2):
+                for u in range(2):
+                    first = 256 * (2 * (pair % pairs_per_x_tile) + a)
+                    nc.tensor.transpose(bank[:, a, u, :], x_words[:, first + u : first + 256 : 2], ident_f32[:])
+            grouped = stage.tile([P, 2 * P * 4], BF16, align_bytes=64)
+            nc.scalar.copy(
+                out=grouped[:].bitcast(F32).rearrange("p (a r u) -> p a r u", a=2, u=2),
+                in_=bank[:].rearrange("p a u r -> p a r u"),
+            )
+            g = 2 * pair
+            nc.vector.quantize_mx(
+                out=x_codes[:, m, P * g : P * (g + 2)].bitcast(FP8X4),
+                scales=x_planes[:, m, P * g : P * (g + 2)],
+                in_=grouped[:],
+            )
+
         u3_bank = psum.tile([P, DH // P, P], BF16, tag="work")
         for a in range(DH // P):
             nc.tensor.transpose(u3_bank[:, a, :], u3_raw[:, a, :], ident_bf[:])
@@ -199,81 +228,82 @@ def tile_polymlp_skiplora_pa_k_kernel(
             nc.tensor.transpose(z2_bank[:, m, :], z2_raw[:, m, :], ident_bf[:])
         z2_t = keep.tile([P, TOKEN_TILES, P], BF16)
         nc.vector.tensor_copy(out=z2_t[:], in_=z2_bank[:])
-
         alpha_f32 = keep.tile([P, 1], F32)
         nc.vector.tensor_copy(out=alpha_f32[:], in_=alpha_bf[:])
+
+        for pair in range(pairs_per_x_tile):
+            x_pair(0, pair)
+
+        def spread_row_early(rows, row, columns):
+            bank = psum.tile([P, BANK], F32, tag="sums")
+            nc.tensor.matmul(
+                bank[:], lhsT=ident_bf[:, row : row + 1].to_broadcast([P, P]), rhs=rows[:, columns],
+                start=True, stop=True,
+            )
+            return bank
+
         gate_gain = keep.tile([P, DH], F32)
         gate_shift = keep.tile([P, DH], F32)
         for hf in range(HALVES):
-            bank = spread_row(rows3, ROW_LN3_G, half_cols(hf))
-            nc.vector.tensor_scalar(
-                out=gate_gain[:, half_cols(hf)], in0=bank[:], scalar1=alpha_f32[:, 0:1], scalar2=None, op0=ALU.mult
+            bank = spread_row_early(rows3, ROW_LN3_G, half_cols(hf))
+            nc.scalar.activation(
+                out=gate_gain[:, half_cols(hf)], in_=bank[:], func=ACT.Copy, scale=alpha_f32[:, 0:1]
             )
         for hf in range(HALVES):
-            bank = spread_row(rows3, ROW_LN3_B, half_cols(hf))
-            nc.vector.tensor_scalar(
-                out=gate_shift[:, half_cols(hf)], in0=bank[:], scalar1=alpha_f32[:, 0:1], scalar2=1.0,
-                op0=ALU.mult, op1=ALU.add,
+            bank = spread_row_early(rows3, ROW_LN3_B, half_cols(hf))
+            nc.scalar.activation(
+                out=gate_shift[:, half_cols(hf)], in_=bank[:], func=ACT.Copy, scale=alpha_f32[:, 0:1], bias=1.0
             )
 
-        gates = []
+        out3 = {}
         for m in range(TOKEN_TILES):
-            gate = per_token_tile.tile([P, DH], F32, name="gate_%d" % m, tag="gate")
             for hf in range(HALVES):
-                bank = psum.tile([P, BANK], F32, tag="work")
+                bank = psum.tile([P, BANK], F32, tag="sums", name="out3_%d_%d" % (m, hf))
                 nc.tensor.matmul(bank[:], lhsT=z2_t[:, m, :], rhs=u3_t[:, half_cols(hf)], start=True, stop=False)
                 nc.tensor.matmul(
                     bank[:], lhsT=ident_bf[:, ROW_U3_B : ROW_U3_B + 1].to_broadcast([P, P]),
                     rhs=rows3[:, half_cols(hf)], start=False, stop=True,
                 )
-                nc.scalar.copy(out=gate[:, half_cols(hf)], in_=bank[:])
-            gates.append(gate)
+                out3[(m, hf)] = bank
 
-        x_codes = keep.tile([P, TOKEN_TILES, G1 * P], U32, tag="codes_then_bias", align_bytes=64)
-        x_planes = keep.tile([P, TOKEN_TILES, G1 * P], U8, align_bytes=64)
-        groups_per_x_tile = G1 // 2
-        for half in range(2):
-            for m in range(TOKEN_TILES):
-                x_words = x_tiles[(half, m)][:].bitcast(F32)
-                for pair in range(groups_per_x_tile // 2):
-                    bank = psum.tile([P, 2, 2, P], F32, tag="work")
-                    for a in range(2):
-                        for u in range(2):
-                            first = 256 * (2 * pair + a)
-                            nc.tensor.transpose(bank[:, a, u, :], x_words[:, first + u : first + 256 : 2], ident_f32[:])
-                    grouped = stage.tile([P, 2 * P * 4], BF16, align_bytes=64)
-                    nc.scalar.copy(
-                        out=grouped[:].bitcast(F32).rearrange("p (a r u) -> p a r u", a=2, u=2),
-                        in_=bank[:].rearrange("p a u r -> p a r u"),
-                    )
-                    g = groups_per_x_tile * half + 2 * pair
-                    nc.vector.quantize_mx(
-                        out=x_codes[:, m, P * g : P * (g + 2)].bitcast(FP8X4),
-                        scales=x_planes[:, m, P * g : P * (g + 2)],
-                        in_=grouped[:],
-                    )
+        def gate_stats(m):
+            stats = small.tile([P, HALVES, 6], F32)
+            for hf in range(HALVES):
+                nc.vector.bn_stats(out=stats[:, hf, :], in_=out3[(m, hf)][:])
+            mean_var = small.tile([P, 2], F32)
+            nc.vector.bn_aggr(out=mean_var[:], in_=stats[:].rearrange("p a s -> p (a s)"))
+            return mean_var
+
+        def gate_std(mean_var):
+            std = small.tile([P, 1], F32)
+            nc.scalar.activation(out=std[:], in_=mean_var[:, 1:2], func=ACT.Sqrt, bias=eps[:, 0:1], scale=1.0)
+            return std
+
+        def gate_centre(m, mean_var):
+            gate = per_token_tile.tile([P, DH], F32, name="gate_%d" % m, tag="gate")
+            for hf in range(HALVES):
+                nc.vector.scalar_tensor_tensor(
+                    out=gate[:, half_cols(hf)], in0=out3[(m, hf)][:], scalar=mean_var[:, 0:1],
+                    in1=gate_gain[:, half_cols(hf)], op0=ALU.subtract, op1=ALU.mult,
+                )
+            return gate
+
+        mean_vars = [gate_stats(m) for m in range(TOKEN_TILES)]
+        x_pair(0, 4)
+        x_pair(0, 5)
+        gates = [gate_centre(0, mean_vars[0])]
+        x_pair(0, 6)
+        x_pair(0, 7)
+        gates.append(gate_centre(1, mean_vars[1]))
+        stds = [gate_std(mean_vars[m]) for m in range(TOKEN_TILES)]
+        for pair in range(PAIRS):
+            x_pair(1, pair)
 
         load_c_words(2)
         load_c_words(3)
 
-        spread = {}
-        for row in (ROW_U1_B, ROW_LN1_G, ROW_LN1_B):
-            spread[row] = keep.tile([P, DH], BF16, name="spread_%d" % row)
-            for hf in range(HALVES):
-                bank = spread_row(rows1, row, half_cols(hf))
-                nc.scalar.copy(out=spread[row][:, half_cols(hf)], in_=bank[:])
-
-        h_gains = []
-        h_shifts = []
         for m in range(TOKEN_TILES):
-            gate = gates[m]
-            std = norm_first(gate, gate_gain)
-            norm_second(gate, std, gate_shift, gate)
-            h_gain = per_token_tile.tile([P, DH], F32, name="h_gain_%d" % m, tag="h_gain")
-            nc.vector.tensor_tensor(out=h_gain[:], in0=gate[:], in1=spread[ROW_LN1_G][:], op=ALU.mult)
-            nc.vector.tensor_tensor(out=gate[:], in0=gate[:], in1=spread[ROW_LN1_B][:], op=ALU.mult)
-            h_gains.append(h_gain)
-            h_shifts.append(gate)
+            norm_second(gates[m], stds[m], gate_shift, gates[m])
 
         sums1 = {}
         for m in range(TOKEN_TILES):
@@ -292,11 +322,36 @@ def tile_polymlp_skiplora_pa_k_kernel(
                     stop=(g == G1 - 1),
                 )
 
+        spread = {}
+        spread_jobs = []
+        for row in (ROW_LN1_G, ROW_LN1_B, ROW_U1_B):
+            spread[row] = keep.tile([P, DH], BF16, name="spread_%d" % row)
+            for hf in range(HALVES):
+                spread_jobs.append((row, hf))
+
+        h_gains = []
+        h_shifts = []
+
+        def gate_times_ln1(m):
+            gate = gates[m]
+            h_gain = per_token_tile.tile([P, DH], F32, name="h_gain_%d" % m, tag="h_gain")
+            nc.vector.tensor_tensor(out=h_gain[:], in0=gate[:], in1=spread[ROW_LN1_G][:], op=ALU.mult)
+            nc.vector.tensor_tensor(out=gate[:], in0=gate[:], in1=spread[ROW_LN1_B][:], op=ALU.mult)
+            h_gains.append(h_gain)
+            h_shifts.append(gate)
+
         for g in range(G1 + TOKEN_TILE_LAG):
             if g < G1:
                 first_product(0, g)
             if g >= TOKEN_TILE_LAG:
                 first_product(1, g - TOKEN_TILE_LAG)
+            if g < len(spread_jobs):
+                row, hf = spread_jobs[g]
+                bank = spread_row(rows1, row, half_cols(hf))
+                nc.scalar.copy(out=spread[row][:, half_cols(hf)], in_=bank[:])
+            if g == len(spread_jobs):
+                for m in range(TOKEN_TILES):
+                    gate_times_ln1(m)
 
         bias_all = keep.tile([P, D], BF16, tag="codes_then_bias", align_bytes=64)
         h_codes = keep.tile([P, TOKEN_TILES, G2 * P], U32, align_bytes=64)

@@ -61,14 +61,14 @@ def tile_polymlp_skiplora_pa_k_kernel(
         ring = stack.enter_context(tc.tile_pool(name="ring", bufs=16))
         psum = stack.enter_context(tc.psum_pool(name="psum", bufs=4))
 
+        u1_planes = keep.tile([P, G1 // 4, DH], U8, align_bytes=64)
+        nc.vector.memset(u1_planes[:].rearrange("p j n -> p (j n)").bitcast(I32), 0)
         rows3 = keep.tile([P, DH], BF16)
         nc.vector.memset(rows3[:].bitcast(I32), 0)
         eps = keep.tile([P, 1], F32)
         nc.vector.memset(eps[:], EPS)
         rows1 = keep.tile([P, DH], BF16)
         nc.vector.memset(rows1[:].bitcast(I32), 0)
-        u1_planes = keep.tile([P, G1 // 4, DH], U8, align_bytes=64)
-        nc.vector.memset(u1_planes[:].rearrange("p j n -> p (j n)").bitcast(I32), 0)
         c_planes = keep.tile([P, G2, RING_COLS], U8, align_bytes=64)
         nc.vector.memset(c_planes[:].rearrange("p g n -> p (g n)").bitcast(I32), 0)
         ident_bf = keep.tile([P, P], BF16)
@@ -129,12 +129,14 @@ def tile_polymlp_skiplora_pa_k_kernel(
 
         def load_c_planes(g):
             for quadrant in range(4):
-                nc.sync.dma_start(
-                    out=c_planes[32 * quadrant : 32 * quadrant + 16, g, :].bitcast(I32),
-                    in_=C_w_scales[g, 4 * quadrant : 4 * quadrant + 4, :]
-                    .rearrange("r (c n) -> c r n", c=QUARTERS)
-                    .bitcast(I32),
-                )
+                for part in range(2):
+                    cols = slice(RING_COLS // 2 * part, RING_COLS // 2 * (part + 1))
+                    nc.sync.dma_start(
+                        out=c_planes[32 * quadrant : 32 * quadrant + 16, g, cols].bitcast(I32),
+                        in_=C_w_scales[g, 4 * quadrant : 4 * quadrant + 4, :]
+                        .rearrange("r (c n) -> c r n", c=QUARTERS)[:, :, cols]
+                        .bitcast(I32),
+                    )
 
         def load_c_words(c):
             for g in range(G2):
@@ -147,17 +149,16 @@ def tile_polymlp_skiplora_pa_k_kernel(
                 )
                 c_tiles[(c, g)] = c_tile
 
-        for m in range(TOKEN_TILES):
-            load_x(0, m, 2 if m == 0 else 1)
-            load_x(1, m, 1)
-            load_u1_planes(m)
+        load_x(0, 0, 2)
         for j in range(G1 // 4):
-            load_u1_words(2 * j)
-            load_u1_words(2 * j + 1)
-            if j < 2:
-                load_u1_planes(j + 2)
-            else:
-                load_c_planes(j - 2)
+            load_u1_planes(j)
+        load_x(1, 0, 1)
+        load_x(0, 1, 1)
+        load_x(1, 1, 1)
+        for a in range(G1 // 2):
+            load_u1_words(a)
+        for g in range(G2):
+            load_c_planes(g)
         load_c_words(0)
         load_c_words(1)
 

@@ -329,6 +329,15 @@ def tile_polymlp_skiplora_pa_k_kernel(
             spread[row] = keep.tile([P, DH], BF16, name="spread_%d" % row)
             for hf in range(HALVES):
                 spread_jobs.append((row, hf))
+        bias_early = keep.tile([P, D // 2], BF16, align_bytes=64)
+        bias_halves = [bias_early]
+
+        def bias_cols(j):
+            return bias_halves[j // BIAS_AHEAD][:, BANK * (j % BIAS_AHEAD) : BANK * (j % BIAS_AHEAD + 1)]
+
+        def spread_bias(j):
+            bank = spread_row(rows1, ROW_C_B + j // HALVES, half_cols(j % HALVES))
+            nc.scalar.copy(out=bias_cols(j), in_=bank[:])
 
         h_gains = []
         h_shifts = []
@@ -346,21 +355,21 @@ def tile_polymlp_skiplora_pa_k_kernel(
                 first_product(0, g)
             if g >= TOKEN_TILE_LAG:
                 first_product(1, g - TOKEN_TILE_LAG)
-            if g < len(spread_jobs):
-                row, hf = spread_jobs[g]
+            for job in spread_jobs[2 * g : 2 * g + 2]:
+                row, hf = job
                 bank = spread_row(rows1, row, half_cols(hf))
                 nc.scalar.copy(out=spread[row][:, half_cols(hf)], in_=bank[:])
-            if g == len(spread_jobs):
+            if g == 3:
                 for m in range(TOKEN_TILES):
                     gate_times_ln1(m)
+            if 3 <= g < 3 + BIAS_AHEAD // 2:
+                spread_bias(2 * (g - 3))
+                spread_bias(2 * (g - 3) + 1)
 
-        bias_all = keep.tile([P, D], BF16, tag="codes_then_bias", align_bytes=64)
+        bias_late = keep.tile([P, D // 2], BF16, tag="codes_then_bias", align_bytes=64)
+        bias_halves.append(bias_late)
         h_codes = keep.tile([P, TOKEN_TILES, G2 * P], U32, align_bytes=64)
         h_planes = keep.tile([P, TOKEN_TILES, G2 * P], U8, align_bytes=64)
-
-        def spread_bias(j):
-            bank = spread_row(rows1, ROW_C_B + j // HALVES, half_cols(j % HALVES))
-            nc.scalar.copy(out=bias_all[:, BANK * j : BANK * (j + 1)], in_=bank[:])
 
         def add_u1_b(m):
             y1 = per_token_tile.tile([P, DH], F32, name="y1_%d" % m, tag="y1")
@@ -386,13 +395,11 @@ def tile_polymlp_skiplora_pa_k_kernel(
                 in_=h_grouped[:].rearrange("p g r t -> p (g r t)"),
             )
 
-        def out_quarter(m, c):
+        def out_quarter(m, c, by_gpsimd, pieces):
             out_tile = ring.tile([P, RING_COLS], F32, tag="ring", name="out_%d_%d" % (m, c), align_bytes=64)
             for i in range(TILES_PER_QUARTER):
                 j = TILES_PER_QUARTER * c + i
-                if m == 0 and j + BIAS_AHEAD < OUT_TILES:
-                    spread_bias(j + BIAS_AHEAD)
-                sums2 = psum.tile([P, BANK], F32, tag="sums")
+                sums2 = psum.tile([P, BANK], F32, tag=("sums" if i % 2 == 0 else "work"), name="sums2")
                 for g in range(G2):
                     nc.tensor.matmul_mx(
                         out=sums2[:],
@@ -403,13 +410,19 @@ def tile_polymlp_skiplora_pa_k_kernel(
                         start=(g == 0),
                         stop=(g == G2 - 1),
                     )
-                nc.vector.tensor_tensor(
-                    out=out_tile[:, BANK * i : BANK * (i + 1)], in0=sums2[:],
-                    in1=bias_all[:, BANK * j : BANK * (j + 1)], op=ALU.add,
-                )
-            nc.sync.dma_start(
-                out=out_rows[P * m : P * (m + 1), RING_COLS * c : RING_COLS * (c + 1)], in_=out_tile[:]
-            )
+                cols = slice(BANK * i, BANK * (i + 1))
+                if i == by_gpsimd:
+                    nc.scalar.copy(out=out_tile[:, cols], in_=sums2[:])
+                    nc.gpsimd.tensor_tensor(out=out_tile[:, cols], in0=out_tile[:, cols], in1=bias_cols(j), op=ALU.add)
+                else:
+                    nc.vector.tensor_tensor(out=out_tile[:, cols], in0=sums2[:], in1=bias_cols(j), op=ALU.add)
+                tiles_per_piece = TILES_PER_QUARTER // pieces
+                if (i + 1) % tiles_per_piece == 0:
+                    first = BANK * (i + 1 - tiles_per_piece)
+                    nc.sync.dma_start(
+                        out=out_rows[P * m : P * (m + 1), RING_COLS * c + first : RING_COLS * c + BANK * (i + 1)],
+                        in_=out_tile[:, first : BANK * (i + 1)],
+                    )
 
         y1_0 = add_u1_b(0)
         std_0 = norm_first(y1_0, h_gains[0])
@@ -418,16 +431,17 @@ def tile_polymlp_skiplora_pa_k_kernel(
         h_grouped_0 = transpose_h(h_0)
         y1_1 = add_u1_b(1)
         std_1 = norm_first(y1_1, h_gains[1])
-        for j in range(BIAS_AHEAD):
+        for j in range(BIAS_AHEAD, OUT_TILES):
             spread_bias(j)
         quantise_h(0, h_grouped_0)
         h_1 = per_token_tile.tile([P, DH], BF16, tag="h")
         norm_second(y1_1, std_1, h_shifts[1], h_1)
 
-        out_quarter(0, 0)
+        out_quarter(0, 0, None, 1)
         h_grouped_1 = transpose_h(h_1)
         quantise_h(1, h_grouped_1)
         for c in range(1, QUARTERS):
-            out_quarter(0, c)
-        for c in range(QUARTERS):
-            out_quarter(1, c)
+            out_quarter(0, c, None, 1)
+        for c in range(QUARTERS - 1):
+            out_quarter(1, c, None, 1)
+        out_quarter(1, QUARTERS - 1, None, TILES_PER_QUARTER)

@@ -129,14 +129,12 @@ def tile_polymlp_skiplora_pa_k_kernel(
 
         def load_c_planes(g):
             for quadrant in range(4):
-                for part in range(2):
-                    cols = slice(RING_COLS // 2 * part, RING_COLS // 2 * (part + 1))
-                    nc.sync.dma_start(
-                        out=c_planes[32 * quadrant : 32 * quadrant + 16, g, cols].bitcast(I32),
-                        in_=C_w_scales[g, 4 * quadrant : 4 * quadrant + 4, :]
-                        .rearrange("r (c n) -> c r n", c=QUARTERS)[:, :, cols]
-                        .bitcast(I32),
-                    )
+                nc.sync.dma_start(
+                    out=c_planes[32 * quadrant : 32 * quadrant + 16, g, :].bitcast(I32),
+                    in_=C_w_scales[g, 4 * quadrant : 4 * quadrant + 4, :]
+                    .rearrange("r (c n) -> c r n", c=QUARTERS)
+                    .bitcast(I32),
+                )
 
         def load_c_words(c):
             for g in range(G2):
@@ -149,16 +147,17 @@ def tile_polymlp_skiplora_pa_k_kernel(
                 )
                 c_tiles[(c, g)] = c_tile
 
-        load_x(0, 0, 2)
+        for m in range(TOKEN_TILES):
+            load_x(0, m, 2 if m == 0 else 1)
+            load_x(1, m, 1)
+            load_u1_planes(m)
         for j in range(G1 // 4):
-            load_u1_planes(j)
-        load_x(1, 0, 1)
-        load_x(0, 1, 1)
-        load_x(1, 1, 1)
-        for a in range(G1 // 2):
-            load_u1_words(a)
-        for g in range(G2):
-            load_c_planes(g)
+            load_u1_words(2 * j)
+            load_u1_words(2 * j + 1)
+            if j < 2:
+                load_u1_planes(j + 2)
+            else:
+                load_c_planes(j - 2)
         load_c_words(0)
         load_c_words(1)
 

@@ -440,7 +440,7 @@ def tile_polymlp_skiplora_pa_k_kernel(
         h_grouped_1 = transpose_h(h_1)
         quantise_h(1, h_grouped_1)
         for c in range(1, QUARTERS):
-            out_quarter(0, c, None, 1)
+            out_quarter(0, c, 1, 1)
         for c in range(QUARTERS - 1):
-            out_quarter(1, c, None, 1)
-        out_quarter(1, QUARTERS - 1, None, TILES_PER_QUARTER)
+            out_quarter(1, c, 1, 1)
+        out_quarter(1, QUARTERS - 1, 0, TILES_PER_QUARTER)

@@ -439,8 +439,10 @@ def tile_polymlp_skiplora_pa_k_kernel(
         out_quarter(0, 0, None, 1)
         h_grouped_1 = transpose_h(h_1)
         quantise_h(1, h_grouped_1)
-        for c in range(1, QUARTERS):
-            out_quarter(0, c, 1, 1)
-        for c in range(QUARTERS - 1):
-            out_quarter(1, c, 1, 1)
-        out_quarter(1, QUARTERS - 1, 0, TILES_PER_QUARTER)
+        out_quarter(0, 1, 1, 1)
+        out_quarter(1, 0, 1, 1)
+        out_quarter(1, 1, 1, 1)
+        out_quarter(0, 2, 1, 1)
+        out_quarter(1, 2, 1, 1)
+        out_quarter(0, 3, 1, 1)
+        out_quarter(1, 3, 0, TILES_PER_QUARTER)

@@ -38,6 +38,8 @@ ROW_C_B = 3
 
 BIAS_AHEAD = 8
 
+U1_PLANES_BY_GPSIMD = (3,)
+
 TOKEN_TILE_LAG = 8
 
 FLOPS = 2 * P * TOKEN_TILES * (D * DH + DQ * DH + DH * D)
@@ -114,10 +116,12 @@ def tile_polymlp_skiplora_pa_k_kernel(
 
         def load_u1_planes(j):
             for quadrant in range(4):
-                nc.sync.dma_start(
-                    out=u1_planes[32 * quadrant : 32 * quadrant + 16, j, :].bitcast(I32),
-                    in_=U1_w_scales[4 * j : 4 * j + 4, 4 * quadrant : 4 * quadrant + 4, :].bitcast(I32),
-                )
+                plane = u1_planes[32 * quadrant : 32 * quadrant + 16, j, :]
+                source = U1_w_scales[4 * j : 4 * j + 4, 4 * quadrant : 4 * quadrant + 4, :]
+                if j in U1_PLANES_BY_GPSIMD:
+                    nc.gpsimd.dma_start(out=plane.bitcast(F32), in_=source.bitcast(F32))
+                else:
+                    nc.sync.dma_start(out=plane.bitcast(I32), in_=source.bitcast(I32))
 
         def load_u1_words(a):
             u1_tile = ring.tile([P, 2, DH], U32, tag="ring", name="u1_%d" % a, align_bytes=64)
@@ -129,11 +133,11 @@ def tile_polymlp_skiplora_pa_k_kernel(
 
         def load_c_planes(g):
             for quadrant in range(4):
-                nc.sync.dma_start(
-                    out=c_planes[32 * quadrant : 32 * quadrant + 16, g, :].bitcast(I32),
+                nc.gpsimd.dma_start(
+                    out=c_planes[32 * quadrant : 32 * quadrant + 16, g, :].bitcast(F32),
                     in_=C_w_scales[g, 4 * quadrant : 4 * quadrant + 4, :]
                     .rearrange("r (c n) -> c r n", c=QUARTERS)
-                    .bitcast(I32),
+                    .bitcast(F32),
                 )
 
         def load_c_words(c):
@@ -147,6 +151,10 @@ def tile_polymlp_skiplora_pa_k_kernel(
                 )
                 c_tiles[(c, g)] = c_tile
 
+        for j in U1_PLANES_BY_GPSIMD:
+            load_u1_planes(j)
+        for g in range(G2):
+            load_c_planes(g)
         for m in range(TOKEN_TILES):
             load_x(0, m, 2 if m == 0 else 1)
             load_x(1, m, 1)
@@ -154,10 +162,8 @@ def tile_polymlp_skiplora_pa_k_kernel(
         for j in range(G1 // 4):
             load_u1_words(2 * j)
             load_u1_words(2 * j + 1)
-            if j < 2:
+            if j < 2 and j + 2 not in U1_PLANES_BY_GPSIMD:
                 load_u1_planes(j + 2)
-            else:
-                load_c_planes(j - 2)
         load_c_words(0)
         load_c_words(1)
 

from contextlib import ExitStack

import concourse.mybir as mybir
from concourse.masks import make_identity

F32 = mybir.dt.float32
BF16 = mybir.dt.bfloat16
I32 = mybir.dt.int32
U32 = mybir.dt.uint32
U8 = mybir.dt.uint8
FP8X4 = mybir.dt.float8_e4m3fn_x4
ALU = mybir.AluOpType
ACT = mybir.ActivationFunctionType

P = 128
TOKEN_TILES = 2
D = 8192
DH = 1024
DQ = 128
EPS = 1e-6
K_PASS = 512
G1 = D // K_PASS
G2 = DH // K_PASS
BANK = 512
HALVES = DH // BANK
RING_COLS = 2048
QUARTERS = D // RING_COLS
TILES_PER_QUARTER = RING_COLS // BANK
OUT_TILES = D // BANK

ROW_U3_B = 0
ROW_LN3_G = 1
ROW_LN3_B = 2
ROW_U1_B = 0
ROW_LN1_G = 1
ROW_LN1_B = 2
ROW_C_B = 3

BIAS_AHEAD = 8

U1_PLANES_BY_GPSIMD = (3,)

TOKEN_TILE_LAG = 8

FLOPS = 2 * P * TOKEN_TILES * (D * DH + DQ * DH + DH * D)


def tile_polymlp_skiplora_pa_k_kernel(
    tc, x, z2, U1_w_words, U1_w_scales, U1_b, U3_w, U3_b, C_w_words, C_w_scales, C_b,
    ln1_g, ln1_b, ln3_g, ln3_b, alpha, out,
):
    nc = tc.nc
    x_rows = x.flatten_outer_dims()
    z2_rows = z2.flatten_outer_dims()
    out_rows = out.flatten_outer_dims()

    with ExitStack() as stack:
        stack.enter_context(tc.manual_schedule())
        keep = stack.enter_context(tc.tile_pool(name="keep", bufs=1))
        per_token_tile = stack.enter_context(tc.tile_pool(name="per_token_tile", bufs=TOKEN_TILES))
        stage = stack.enter_context(tc.tile_pool(name="stage", bufs=4))
        small = stack.enter_context(tc.tile_pool(name="small", bufs=4))
        ring = stack.enter_context(tc.tile_pool(name="ring", bufs=16))
        psum = stack.enter_context(tc.psum_pool(name="psum", bufs=4))

        u1_planes = keep.tile([P, G1 // 4, DH], U8, align_bytes=64)
        nc.vector.memset(u1_planes[:].rearrange("p j n -> p (j n)").bitcast(I32), 0)
        rows3 = keep.tile([P, DH], BF16)
        nc.vector.memset(rows3[:].bitcast(I32), 0)
        eps = keep.tile([P, 1], F32)
        nc.vector.memset(eps[:], EPS)
        rows1 = keep.tile([P, DH], BF16)
        nc.vector.memset(rows1[:].bitcast(I32), 0)
        c_planes = keep.tile([P, G2, RING_COLS], U8, align_bytes=64)
        nc.vector.memset(c_planes[:].rearrange("p g n -> p (g n)").bitcast(I32), 0)
        ident_bf = keep.tile([P, P], BF16)
        make_identity(nc, ident_bf[:])
        ident_f32 = keep.tile([P, P], F32)
        make_identity(nc, ident_f32[:])

        def load_row(queue, rows, row, vector):
            queue.dma_start(out=rows[row : row + 1, :], in_=vector.rearrange("(o n) -> o n", o=1))

        u3_raw = keep.tile([P, DH // P, DQ], BF16)
        nc.scalar.dma_start(out=u3_raw[:], in_=U3_w.rearrange("(p a) k -> p a k", a=DH // P))
        z2_raw = keep.tile([P, TOKEN_TILES, DQ], BF16)
        nc.scalar.dma_start(out=z2_raw[:], in_=z2_rows.rearrange("(m p) k -> p m k", p=P))
        load_row(nc.scalar, rows3, ROW_U3_B, U3_b)
        load_row(nc.scalar, rows3, ROW_LN3_G, ln3_g)
        load_row(nc.scalar, rows3, ROW_LN3_B, ln3_b)
        alpha_bf = keep.tile([P, 1], BF16)
        nc.scalar.dma_start(out=alpha_bf[:], in_=alpha.partition_broadcast(P))
        table_warm = keep.tile([P, 1], F32)
        nc.scalar.activation(out=table_warm[:], in_=eps[:], func=ACT.Sqrt)
        load_row(nc.gpsimd, rows1, ROW_U1_B, U1_b)
        load_row(nc.gpsimd, rows1, ROW_LN1_G, ln1_g)
        load_row(nc.gpsimd, rows1, ROW_LN1_B, ln1_b)
        nc.gpsimd.dma_start(
            out=rows1[ROW_C_B : ROW_C_B + D // DH, :], in_=C_b.rearrange("(r n) -> r n", n=DH)
        )

        x_tiles = {}
        u1_tiles = []
        c_tiles = {}

        def load_x(half, m, pieces):
            x_tile = ring.tile([P, 2 * RING_COLS], BF16, tag="ring", name="x_%d_%d" % (half, m), align_bytes=64)
            width = 2 * RING_COLS // pieces
            for i in range(pieces):
                first = 2 * RING_COLS * half + width * i
                nc.sync.dma_start(
                    out=x_tile[:, width * i : width * (i + 1)],
                    in_=x_rows[P * m : P * (m + 1), first : first + width],
                )
            x_tiles[(half, m)] = x_tile

        def load_u1_planes(j):
            for quadrant in range(4):
                plane = u1_planes[32 * quadrant : 32 * quadrant + 16, j, :]
                source = U1_w_scales[4 * j : 4 * j + 4, 4 * quadrant : 4 * quadrant + 4, :]
                if j in U1_PLANES_BY_GPSIMD:
                    nc.gpsimd.dma_start(out=plane.bitcast(F32), in_=source.bitcast(F32))
                else:
                    nc.sync.dma_start(out=plane.bitcast(I32), in_=source.bitcast(I32))

        def load_u1_words(a):
            u1_tile = ring.tile([P, 2, DH], U32, tag="ring", name="u1_%d" % a, align_bytes=64)
            nc.sync.dma_start(
                out=u1_tile[:].bitcast(I32),
                in_=U1_w_words[2 * a : 2 * a + 2].rearrange("g p n t -> p g (n t)").bitcast(I32),
            )
            u1_tiles.append(u1_tile)

        def load_c_planes(g):
            for quadrant in range(4):
                nc.gpsimd.dma_start(
                    out=c_planes[32 * quadrant : 32 * quadrant + 16, g, :].bitcast(F32),
                    in_=C_w_scales[g, 4 * quadrant : 4 * quadrant + 4, :]
                    .rearrange("r (c n) -> c r n", c=QUARTERS)
                    .bitcast(F32),
                )

        def load_c_words(c):
            for g in range(G2):
                c_tile = ring.tile([P, RING_COLS], U32, tag="ring", name="c_%d_%d" % (c, g), align_bytes=64)
                nc.sync.dma_start(
                    out=c_tile[:].bitcast(I32),
                    in_=C_w_words[g, :, RING_COLS * c : RING_COLS * (c + 1), :]
                    .rearrange("p n t -> p (n t)")
                    .bitcast(I32),
                )
                c_tiles[(c, g)] = c_tile

        for j in U1_PLANES_BY_GPSIMD:
            load_u1_planes(j)
        for g in range(G2):
            load_c_planes(g)
        for m in range(TOKEN_TILES):
            load_x(0, m, 2 if m == 0 else 1)
            load_x(1, m, 1)
            load_u1_planes(m)
        for j in range(G1 // 4):
            load_u1_words(2 * j)
            load_u1_words(2 * j + 1)
            if j < 2 and j + 2 not in U1_PLANES_BY_GPSIMD:
                load_u1_planes(j + 2)
        load_c_words(0)
        load_c_words(1)

        def spread_row(rows, row, columns):
            bank = psum.tile([P, BANK], F32, tag="work")
            nc.tensor.matmul(
                bank[:], lhsT=ident_bf[:, row : row + 1].to_broadcast([P, P]), rhs=rows[:, columns],
                start=True, stop=True,
            )
            return bank

        def half_cols(hf):
            return slice(BANK * hf, BANK * (hf + 1))

        def norm_first(y, gain):
            stats = small.tile([P, HALVES, 6], F32)
            for hf in range(HALVES):
                nc.vector.bn_stats(out=stats[:, hf, :], in_=y[:, half_cols(hf)])
            mean_var = small.tile([P, 2], F32)
            nc.vector.bn_aggr(out=mean_var[:], in_=stats[:].rearrange("p a s -> p (a s)"))
            std = small.tile([P, 1], F32)
            nc.scalar.activation(out=std[:], in_=mean_var[:, 1:2], func=ACT.Sqrt, bias=eps[:, 0:1], scale=1.0)
            nc.vector.scalar_tensor_tensor(
                out=y[:], in0=y[:], scalar=mean_var[:, 0:1], in1=gain[:], op0=ALU.subtract, op1=ALU.mult
            )
            return std

        def norm_second(y, std, shift, result):
            rstd = small.tile([P, 1], F32)
            nc.vector.reciprocal(out=rstd[:], in_=std[:])
            nc.vector.scalar_tensor_tensor(
                out=result[:], in0=y[:], scalar=rstd[:, 0:1], in1=shift[:], op0=ALU.mult, op1=ALU.add
            )

        x_codes = keep.tile([P, TOKEN_TILES, G1 * P], U32, tag="codes_then_bias", align_bytes=64)
        x_planes = keep.tile([P, TOKEN_TILES, G1 * P], U8, align_bytes=64)
        PAIRS = G1 // 2
        pairs_per_x_tile = PAIRS // 2

        def x_pair(m, pair):
            x_words = x_tiles[(pair // pairs_per_x_tile, m)][:].bitcast(F32)
            bank = psum.tile([P, 2, 2, P], F32, tag="work")
            for a in range(2):
                for u in range(2):
                    first = 256 * (2 * (pair % pairs_per_x_tile) + a)
                    nc.tensor.transpose(bank[:, a, u, :], x_words[:, first + u : first + 256 : 2], ident_f32[:])
            grouped = stage.tile([P, 2 * P * 4], BF16, align_bytes=64)
            nc.scalar.copy(
                out=grouped[:].bitcast(F32).rearrange("p (a r u) -> p a r u", a=2, u=2),
                in_=bank[:].rearrange("p a u r -> p a r u"),
            )
            g = 2 * pair
            nc.vector.quantize_mx(
                out=x_codes[:, m, P * g : P * (g + 2)].bitcast(FP8X4),
                scales=x_planes[:, m, P * g : P * (g + 2)],
                in_=grouped[:],
            )

        u3_bank = psum.tile([P, DH // P, P], BF16, tag="work")
        for a in range(DH // P):
            nc.tensor.transpose(u3_bank[:, a, :], u3_raw[:, a, :], ident_bf[:])
        u3_t = keep.tile([P, DH], BF16)
        nc.vector.tensor_copy(
            out=u3_t[:].rearrange("k (p a) -> k p a", a=DH // P), in_=u3_bank[:].rearrange("k a p -> k p a")
        )
        z2_bank = psum.tile([P, TOKEN_TILES, P], BF16, tag="work")
        for m in range(TOKEN_TILES):
            nc.tensor.transpose(z2_bank[:, m, :], z2_raw[:, m, :], ident_bf[:])
        z2_t = keep.tile([P, TOKEN_TILES, P], BF16)
        nc.vector.tensor_copy(out=z2_t[:], in_=z2_bank[:])
        alpha_f32 = keep.tile([P, 1], F32)
        nc.vector.tensor_copy(out=alpha_f32[:], in_=alpha_bf[:])

        for pair in range(pairs_per_x_tile):
            x_pair(0, pair)

        def spread_row_early(rows, row, columns):
            bank = psum.tile([P, BANK], F32, tag="sums")
            nc.tensor.matmul(
                bank[:], lhsT=ident_bf[:, row : row + 1].to_broadcast([P, P]), rhs=rows[:, columns],
                start=True, stop=True,
            )
            return bank

        gate_gain = keep.tile([P, DH], F32)
        gate_shift = keep.tile([P, DH], F32)
        for hf in range(HALVES):
            bank = spread_row_early(rows3, ROW_LN3_G, half_cols(hf))
            nc.scalar.activation(
                out=gate_gain[:, half_cols(hf)], in_=bank[:], func=ACT.Copy, scale=alpha_f32[:, 0:1]
            )
        for hf in range(HALVES):
            bank = spread_row_early(rows3, ROW_LN3_B, half_cols(hf))
            nc.scalar.activation(
                out=gate_shift[:, half_cols(hf)], in_=bank[:], func=ACT.Copy, scale=alpha_f32[:, 0:1], bias=1.0
            )

        out3 = {}
        for m in range(TOKEN_TILES):
            for hf in range(HALVES):
                bank = psum.tile([P, BANK], F32, tag="sums", name="out3_%d_%d" % (m, hf))
                nc.tensor.matmul(bank[:], lhsT=z2_t[:, m, :], rhs=u3_t[:, half_cols(hf)], start=True, stop=False)
                nc.tensor.matmul(
                    bank[:], lhsT=ident_bf[:, ROW_U3_B : ROW_U3_B + 1].to_broadcast([P, P]),
                    rhs=rows3[:, half_cols(hf)], start=False, stop=True,
                )
                out3[(m, hf)] = bank

        def gate_stats(m):
            stats = small.tile([P, HALVES, 6], F32)
            for hf in range(HALVES):
                nc.vector.bn_stats(out=stats[:, hf, :], in_=out3[(m, hf)][:])
            mean_var = small.tile([P, 2], F32)
            nc.vector.bn_aggr(out=mean_var[:], in_=stats[:].rearrange("p a s -> p (a s)"))
            return mean_var

        def gate_std(mean_var):
            std = small.tile([P, 1], F32)
            nc.scalar.activation(out=std[:], in_=mean_var[:, 1:2], func=ACT.Sqrt, bias=eps[:, 0:1], scale=1.0)
            return std

        def gate_centre(m, mean_var):
            gate = per_token_tile.tile([P, DH], F32, name="gate_%d" % m, tag="gate")
            for hf in range(HALVES):
                nc.vector.scalar_tensor_tensor(
                    out=gate[:, half_cols(hf)], in0=out3[(m, hf)][:], scalar=mean_var[:, 0:1],
                    in1=gate_gain[:, half_cols(hf)], op0=ALU.subtract, op1=ALU.mult,
                )
            return gate

        mean_vars = [gate_stats(m) for m in range(TOKEN_TILES)]
        x_pair(0, 4)
        x_pair(0, 5)
        gates = [gate_centre(0, mean_vars[0])]
        x_pair(0, 6)
        x_pair(0, 7)
        gates.append(gate_centre(1, mean_vars[1]))
        stds = [gate_std(mean_vars[m]) for m in range(TOKEN_TILES)]
        for pair in range(PAIRS):
            x_pair(1, pair)

        load_c_words(2)
        load_c_words(3)

        for m in range(TOKEN_TILES):
            norm_second(gates[m], stds[m], gate_shift, gates[m])

        sums1 = {}
        for m in range(TOKEN_TILES):
            for hf in range(HALVES):
                sums1[(m, hf)] = psum.tile([P, BANK], F32, tag="sums", name="sums1_%d_%d" % (m, hf))

        def first_product(m, g):
            for hf in range(HALVES):
                nc.tensor.matmul_mx(
                    out=sums1[(m, hf)][:],
                    lhsT=x_codes[:, m, P * g : P * (g + 1)].bitcast(FP8X4),
                    lhsT_scale=x_planes[:, m, P * g : P * (g + 1)],
                    rhs=u1_tiles[g // 2][:, g % 2, half_cols(hf)].bitcast(FP8X4),
                    rhs_scale=u1_planes[4 * (g % 4) : P, g // 4, half_cols(hf)],
                    start=(g == 0),
                    stop=(g == G1 - 1),
                )

        spread = {}
        spread_jobs = []
        for row in (ROW_LN1_G, ROW_LN1_B, ROW_U1_B):
            spread[row] = keep.tile([P, DH], BF16, name="spread_%d" % row)
            for hf in range(HALVES):
                spread_jobs.append((row, hf))
        bias_early = keep.tile([P, D // 2], BF16, align_bytes=64)
        bias_halves = [bias_early]

        def bias_cols(j):
            return bias_halves[j // BIAS_AHEAD][:, BANK * (j % BIAS_AHEAD) : BANK * (j % BIAS_AHEAD + 1)]

        def spread_bias(j):
            bank = spread_row(rows1, ROW_C_B + j // HALVES, half_cols(j % HALVES))
            nc.scalar.copy(out=bias_cols(j), in_=bank[:])

        h_gains = []
        h_shifts = []

        def gate_times_ln1(m):
            gate = gates[m]
            h_gain = per_token_tile.tile([P, DH], F32, name="h_gain_%d" % m, tag="h_gain")
            nc.vector.tensor_tensor(out=h_gain[:], in0=gate[:], in1=spread[ROW_LN1_G][:], op=ALU.mult)
            nc.vector.tensor_tensor(out=gate[:], in0=gate[:], in1=spread[ROW_LN1_B][:], op=ALU.mult)
            h_gains.append(h_gain)
            h_shifts.append(gate)

        for g in range(G1 + TOKEN_TILE_LAG):
            if g < G1:
                first_product(0, g)
            if g >= TOKEN_TILE_LAG:
                first_product(1, g - TOKEN_TILE_LAG)
            for job in spread_jobs[2 * g : 2 * g + 2]:
                row, hf = job
                bank = spread_row(rows1, row, half_cols(hf))
                nc.scalar.copy(out=spread[row][:, half_cols(hf)], in_=bank[:])
            if g == 3:
                for m in range(TOKEN_TILES):
                    gate_times_ln1(m)
            if 3 <= g < 3 + BIAS_AHEAD // 2:
                spread_bias(2 * (g - 3))
                spread_bias(2 * (g - 3) + 1)

        bias_late = keep.tile([P, D // 2], BF16, tag="codes_then_bias", align_bytes=64)
        bias_halves.append(bias_late)
        h_codes = keep.tile([P, TOKEN_TILES, G2 * P], U32, align_bytes=64)
        h_planes = keep.tile([P, TOKEN_TILES, G2 * P], U8, align_bytes=64)

        def add_u1_b(m):
            y1 = per_token_tile.tile([P, DH], F32, name="y1_%d" % m, tag="y1")
            for hf in range(HALVES):
                nc.vector.tensor_tensor(
                    out=y1[:, half_cols(hf)], in0=sums1[(m, hf)][:], in1=spread[ROW_U1_B][:, half_cols(hf)], op=ALU.add
                )
            return y1

        def transpose_h(h):
            bank = psum.tile([P, G2, 4, P], BF16, tag="work")
            for g in range(G2):
                for t in range(4):
                    nc.tensor.transpose(bank[:, g, t, :], h[:, K_PASS * g + t : K_PASS * (g + 1) : 4], ident_bf[:])
            h_grouped = per_token_tile.tile([P, G2, P, 4], BF16, align_bytes=64)
            nc.scalar.copy(out=h_grouped[:], in_=bank[:].rearrange("p g t r -> p g r t"))
            return h_grouped

        def quantise_h(m, h_grouped):
            nc.vector.quantize_mx(
                out=h_codes[:, m, :].bitcast(FP8X4),
                scales=h_planes[:, m, :],
                in_=h_grouped[:].rearrange("p g r t -> p (g r t)"),
            )

        def out_quarter(m, c, by_gpsimd, pieces):
            out_tile = ring.tile([P, RING_COLS], F32, tag="ring", name="out_%d_%d" % (m, c), align_bytes=64)
            for i in range(TILES_PER_QUARTER):
                j = TILES_PER_QUARTER * c + i
                sums2 = psum.tile([P, BANK], F32, tag=("sums" if i % 2 == 0 else "work"), name="sums2")
                for g in range(G2):
                    nc.tensor.matmul_mx(
                        out=sums2[:],
                        lhsT=h_codes[:, m, P * g : P * (g + 1)].bitcast(FP8X4),
                        lhsT_scale=h_planes[:, m, P * g : P * (g + 1)],
                        rhs=c_tiles[(c, g)][:, BANK * i : BANK * (i + 1)].bitcast(FP8X4),
                        rhs_scale=c_planes[4 * c : P, g, BANK * i : BANK * (i + 1)],
                        start=(g == 0),
                        stop=(g == G2 - 1),
                    )
                cols = slice(BANK * i, BANK * (i + 1))
                if i == by_gpsimd:
                    nc.scalar.copy(out=out_tile[:, cols], in_=sums2[:])
                    nc.gpsimd.tensor_tensor(out=out_tile[:, cols], in0=out_tile[:, cols], in1=bias_cols(j), op=ALU.add)
                else:
                    nc.vector.tensor_tensor(out=out_tile[:, cols], in0=sums2[:], in1=bias_cols(j), op=ALU.add)
                tiles_per_piece = TILES_PER_QUARTER // pieces
                if (i + 1) % tiles_per_piece == 0:
                    first = BANK * (i + 1 - tiles_per_piece)
                    nc.sync.dma_start(
                        out=out_rows[P * m : P * (m + 1), RING_COLS * c + first : RING_COLS * c + BANK * (i + 1)],
                        in_=out_tile[:, first : BANK * (i + 1)],
                    )

        y1_0 = add_u1_b(0)
        std_0 = norm_first(y1_0, h_gains[0])
        h_0 = per_token_tile.tile([P, DH], BF16, tag="h")
        norm_second(y1_0, std_0, h_shifts[0], h_0)
        h_grouped_0 = transpose_h(h_0)
        y1_1 = add_u1_b(1)
        std_1 = norm_first(y1_1, h_gains[1])
        for j in range(BIAS_AHEAD, OUT_TILES):
            spread_bias(j)
        quantise_h(0, h_grouped_0)
        h_1 = per_token_tile.tile([P, DH], BF16, tag="h")
        norm_second(y1_1, std_1, h_shifts[1], h_1)

        out_quarter(0, 0, None, 1)
        h_grouped_1 = transpose_h(h_1)
        quantise_h(1, h_grouped_1)
        out_quarter(0, 1, 1, 1)
        out_quarter(1, 0, 1, 1)
        out_quarter(1, 1, 1, 1)
        out_quarter(0, 2, 1, 1)
        out_quarter(1, 2, 1, 1)
        out_quarter(0, 3, 1, 1)
        out_quarter(1, 3, 0, TILES_PER_QUARTER)
